import numpy as np
import ml_dtypes


def mxq(x, axis, fmt="e4m3"):
    dtype, down = {"e4m3": (ml_dtypes.float8_e4m3fn, 7), "e5m2": (ml_dtypes.float8_e5m2, 14)}[fmt]
    v = np.moveaxis(np.asarray(x, np.float32).astype(ml_dtypes.bfloat16).astype(np.float64), axis, -1)
    blocks = v.reshape(v.shape[:-1] + (-1, 32))
    amax = np.abs(blocks).max(-1, keepdims=True)
    byte = np.maximum(np.where(amax > 0, np.frexp(amax)[1] - 1 + 127, 0) - down, 1)
    scale = np.exp2(byte - 127.0)
    codes = (blocks / scale).astype(np.float32).astype(dtype).astype(np.float64)
    return np.moveaxis((codes * scale).reshape(v.shape), -1, axis)


WIDE = False


def mx_kscale(k):
    if not WIDE:
        return np.ones(k)
    levels = np.array([10, -10, 5, -5, 0])
    a = np.random.permutation(np.resize(levels, k // 512 * 4)).reshape(k // 512, 4)
    idx = np.arange(k)
    return np.exp2(a[idx // 512, idx % 128 // 32])


BF16 = ml_dtypes.bfloat16


def bf(x):
    return np.asarray(x, np.float32).astype(BF16)


def f64(x):
    return np.asarray(x).astype(np.float64)


E2M1 = np.array([0.0, 0.5, 1.0, 1.5, 2.0, 3.0, 4.0, 6.0, -0.0, -0.5, -1.0, -1.5, -2.0, -3.0, -4.0, -6.0])


def pack_weight(w, fmt):
    k, n = w.shape
    w = f64(bf(w)).reshape(k // 32, 32, n)
    amax = np.abs(w).max(1)
    if fmt == "e4m3":
        byte = np.frexp(amax)[1] - 1 + 127 - 7
    else:
        mant, ex = np.frexp(amax / 6.0)
        byte = np.where(mant > 0.5, ex, ex - 1) + 127
    byte = np.clip(np.where(amax > 0, byte, 1), 1, 254)
    scaled = (w * np.exp2(127.0 - byte)[:, None, :]).reshape(k, n).astype(np.float32)
    by_word = np.ascontiguousarray(scaled.reshape(k // 512, 128, 4, n).transpose(0, 1, 3, 2))
    if fmt == "e4m3":
        words = by_word.astype(ml_dtypes.float8_e4m3fn).view(np.uint8)
    else:
        c = by_word.astype(ml_dtypes.float4_e2m1fn).view(np.uint8) & 0xF
        words = c[..., 0::2] | (c[..., 1::2] << 4)
    return np.ascontiguousarray(words), np.ascontiguousarray(byte.astype(np.uint8).reshape(k // 512, 16, n))


def unpack_weight(words, scales, fmt):
    g, p, n, _ = words.shape
    if fmt == "e4m3":
        vals = np.ascontiguousarray(words).view(ml_dtypes.float8_e4m3fn).astype(np.float64)
    else:
        nib = np.empty((g, p, n, 4), np.uint8)
        nib[..., 0::2] = words & 0xF
        nib[..., 1::2] = words >> 4
        vals = E2M1[nib]
    vals = vals * np.repeat(np.exp2(scales.astype(np.float64) - 127.0), 8, axis=1)[..., None]
    return vals.transpose(0, 1, 3, 2).reshape(g * 512, n)


T, DIM, H, HKV, D = 128, 8192, 16, 4, 128
THETA = 10000.0
NQ, NK = H * D, HKV * D


def rope(u):
    inv_freq = 1.0 / THETA ** (np.arange(0, D, 2) / D)
    ang = np.arange(T)[:, None] * inv_freq
    cos, sin = np.cos(ang)[:, None, :], np.sin(ang)[:, None, :]
    p = u.reshape(T, -1, D // 2, 2)
    u1, u2 = p[..., 0], p[..., 1]
    return np.stack([u1 * cos - u2 * sin, u1 * sin + u2 * cos], axis=-1).reshape(u.shape)


def setup_inputs():
    s = mx_kscale(DIM)
    x = bf(np.random.standard_normal((T, DIM)) * s)
    words, scales = pack_weight((np.random.standard_normal((NQ + NK + NK, DIM)) / np.sqrt(DIM) / s).T, "e4m3")
    return {"x": x, "w_qkv_words": words, "w_qkv_scales": scales}


def reference(x, w_qkv_words, w_qkv_scales):
    qkv = mxq(f64(x), 1, "e4m3") @ unpack_weight(w_qkv_words, w_qkv_scales, "e4m3")
    q = qkv[:, :NQ].reshape(T, H, D)
    k = qkv[:, NQ:NQ + NK].reshape(T, HKV, D)
    v = qkv[:, NQ + NK:].reshape(T, HKV, D)
    return rope(q), rope(k), v

@@ -1,0 +1,235 @@
+import math
+from contextlib import ExitStack
+
+import concourse.mybir as mybir
+from concourse.masks import make_identity
+
+F32 = mybir.dt.float32
+BF16 = mybir.dt.bfloat16
+I32 = mybir.dt.int32
+U32 = mybir.dt.uint32
+U8 = mybir.dt.uint8
+FP8X4 = mybir.dt.float8_e4m3fn_x4
+ALU = mybir.AluOpType
+
+P = 128
+DIM = 8192
+K_PASS = 512
+GROUPS = DIM // K_PASS
+D = 128
+HALF = D // 2
+DOUBLINGS = 6
+BANK = 512
+HEADS_PER_BANK = BANK // D
+N_ALL = 3072
+N_ROT = 2560
+ROT_BANKS = N_ROT // BANK
+THETA = 10000.0
+
+X_CHUNKS = 4
+GROUPS_PER_CHUNK = GROUPS // X_CHUNKS
+GROUPS_PER_FILL = 2
+FILLS = GROUPS // GROUPS_PER_FILL
+PLANES_PER_TILE = 4
+PLANE_TILES = GROUPS // PLANES_PER_TILE
+QK_BUFS = 8
+V_GROUPS_PER_LOAD = 2
+V_LOADS = GROUPS // V_GROUPS_PER_LOAD
+
+TWO_PI = 2.0 * math.pi
+TWO_PI_HIGH = 6.28125
+TWO_PI_LOW = TWO_PI - TWO_PI_HIGH
+ROUND_MAGIC = 12582912.0
+
+FLOPS = 2 * P * DIM * N_ALL
+
+
+def tile_attention_pa_k_kernel(tc, x, w_qkv_words, w_qkv_scales, out_0, out_1, out_2):
+    nc = tc.nc
+    with ExitStack() as ctx:
+        ctx.enter_context(tc.manual_schedule())
+        const = ctx.enter_context(tc.tile_pool(name="const", bufs=1))
+        x_pool = ctx.enter_context(tc.tile_pool(name="x_pool", bufs=X_CHUNKS))
+        grouped_pool = ctx.enter_context(tc.tile_pool(name="grouped_pool", bufs=4))
+        qk_pool = ctx.enter_context(tc.tile_pool(name="qk_pool", bufs=QK_BUFS))
+        v_pool = ctx.enter_context(tc.tile_pool(name="v_pool", bufs=V_LOADS))
+        prod_pool = ctx.enter_context(tc.tile_pool(name="prod_pool", bufs=2))
+        out_pool = ctx.enter_context(tc.tile_pool(name="out_pool", bufs=ROT_BANKS + 1))
+        xt_psum = ctx.enter_context(tc.psum_pool(name="xt_psum", bufs=2))
+        acc_psum = ctx.enter_context(tc.psum_pool(name="acc_psum", bufs=1))
+
+        x_chunks = []
+        chunk_cols = GROUPS_PER_CHUNK * K_PASS
+        for c in range(X_CHUNKS):
+            x_chunk = x_pool.tile([P, chunk_cols], BF16, name="x_chunk")
+            nc.sync.dma_start(out=x_chunk[:], in_=x[:, c * chunk_cols : (c + 1) * chunk_cols])
+            x_chunks.append(x_chunk)
+
+        plane_tiles = []
+        for j in range(PLANE_TILES):
+            planes = const.tile([P, N_ALL], U8, name="planes%d" % j, align_bytes=64)
+            nc.vector.memset(planes[:].bitcast(I32), 0)
+            plane_tiles.append(planes)
+        for j in range(PLANE_TILES):
+            for quadrant in range(4):
+                nc.sync.dma_start(
+                    out=plane_tiles[j][32 * quadrant : 32 * quadrant + 16, :].bitcast(I32),
+                    in_=w_qkv_scales[
+                        PLANES_PER_TILE * j : PLANES_PER_TILE * (j + 1), 4 * quadrant : 4 * quadrant + 4, :
+                    ].bitcast(I32),
+                )
+
+        def load_qk(g):
+            w_qk = qk_pool.tile([P, N_ROT], U32, name="w_qk", align_bytes=64)
+            words = w_qkv_words[g].rearrange("p n t -> p (n t)")
+            nc.sync.dma_start(out=w_qk[:].bitcast(I32), in_=words[:, 0 : 4 * N_ROT].bitcast(I32))
+            return w_qk
+
+        def load_v(i):
+            w_v = v_pool.tile([P, V_GROUPS_PER_LOAD, BANK], U32, name="w_v", align_bytes=64)
+            words = w_qkv_words[V_GROUPS_PER_LOAD * i : V_GROUPS_PER_LOAD * (i + 1)].rearrange(
+                "g p n t -> p g (n t)"
+            )
+            nc.sync.dma_start(out=w_v[:].bitcast(I32), in_=words[:, :, 4 * N_ROT : 4 * N_ALL].bitcast(I32))
+            return w_v
+
+        qk_tiles = [load_qk(g) for g in range(QK_BUFS)]
+        v_tiles = []
+
+        ident = const.tile([P, P], F32, name="ident")
+        make_identity(nc, ident[:])
+        x_codes = const.tile([P, GROUPS * P], U32, name="x_codes", align_bytes=64)
+        x_scales = const.tile([P, GROUPS * P], U8, name="x_scales", align_bytes=64)
+        fill_cols = GROUPS_PER_FILL * P
+
+        def quantise_fill(b, grouped):
+            cols = slice(b * fill_cols, (b + 1) * fill_cols)
+            nc.vector.quantize_mx(out=x_codes[:, cols].bitcast(FP8X4), scales=x_scales[:, cols], in_=grouped[:])
+
+        previous = None
+        for b in range(FILLS):
+            xt = xt_psum.tile([P, GROUPS_PER_FILL, 2, P], F32, name="xt")
+            for i in range(GROUPS_PER_FILL):
+                g = GROUPS_PER_FILL * b + i
+                words = x_chunks[g // GROUPS_PER_CHUNK][:].bitcast(F32)
+                first = (g % GROUPS_PER_CHUNK) * (K_PASS // 2)
+                for u in range(2):
+                    nc.tensor.transpose(
+                        xt[:, i, u, :], words[:, first + u : first + K_PASS // 2 : 2], ident[:]
+                    )
+            grouped = grouped_pool.tile([P, 4 * fill_cols], BF16, name="grouped", align_bytes=64)
+            grouped_words = grouped[:].bitcast(F32).rearrange("p (i r u) -> p i r u", i=GROUPS_PER_FILL, u=2)
+            xt_words = xt[:].rearrange("p i u r -> p i r u")
+            if b % 2 == 0:
+                nc.vector.tensor_copy(out=grouped_words, in_=xt_words)
+            else:
+                nc.scalar.copy(out=grouped_words, in_=xt_words)
+            if previous is not None:
+                quantise_fill(b - 1, previous)
+            previous = grouped
+        quantise_fill(FILLS - 1, previous)
+
+        pos_int = const.tile([P, 1], I32, name="pos_int")
+        nc.gpsimd.iota(pos_int[:], pattern=[[0, 1]], base=0, channel_multiplier=1)
+        pos = const.tile([P, 1], F32, name="pos")
+        nc.vector.tensor_copy(out=pos[:], in_=pos_int[:])
+        neg_pos = const.tile([P, 1], F32, name="neg_pos")
+        nc.vector.tensor_scalar(out=neg_pos[:], in0=pos[:], scalar1=-1.0, scalar2=None, op0=ALU.mult)
+        freq = const.tile([P, HALF], F32, name="freq")
+        nc.vector.memset(freq[:, 0:1], 1.0)
+        for doubling in range(DOUBLINGS):
+            span = 2**doubling
+            nc.vector.tensor_scalar(
+                out=freq[:, span : 2 * span],
+                in0=freq[:, 0:span],
+                scalar1=THETA ** (-2.0 * span / D),
+                scalar2=None,
+                op0=ALU.mult,
+            )
+        angle = const.tile([P, 2, HALF, 2], F32, name="angle")
+
+        def angle_plane(row, col, position, shift):
+            nc.vector.tensor_scalar(
+                out=angle[:, row, :, col],
+                in0=freq[:],
+                scalar1=position[:],
+                scalar2=shift,
+                op0=ALU.mult,
+                op1=ALU.add,
+            )
+
+        angle_plane(0, 0, pos, math.pi / 2)
+        angle_plane(0, 1, neg_pos, 0.0)
+        angle_plane(1, 0, pos, 0.0)
+        angle_plane(1, 1, pos, math.pi / 2)
+        angle_flat = angle[:].rearrange("p a i b -> p (a i b)")
+        turns = const.tile([P, 4 * HALF], F32, name="turns")
+        nc.vector.tensor_scalar(
+            out=turns[:], in0=angle_flat, scalar1=1.0 / TWO_PI, scalar2=ROUND_MAGIC, op0=ALU.mult, op1=ALU.add
+        )
+        nc.vector.tensor_scalar(out=turns[:], in0=turns[:], scalar1=ROUND_MAGIC, scalar2=None, op0=ALU.subtract)
+        reduced_high = const.tile([P, 4 * HALF], F32, name="reduced_high")
+        nc.vector.scalar_tensor_tensor(
+            out=reduced_high[:], in0=turns[:], scalar=-TWO_PI_HIGH, in1=angle_flat, op0=ALU.mult, op1=ALU.add
+        )
+        reduced = const.tile([P, 4 * HALF], F32, name="reduced")
+        nc.vector.scalar_tensor_tensor(
+            out=reduced[:], in0=turns[:], scalar=-TWO_PI_LOW, in1=reduced_high[:], op0=ALU.mult, op1=ALU.add
+        )
+        rotation = const.tile([P, 2, D], F32, name="rotation")
+        nc.scalar.activation(
+            out=rotation[:].rearrange("p a c -> p (a c)"), in_=reduced[:], func=mybir.ActivationFunctionType.Sin
+        )
+
+        acc = [acc_psum.tile([P, BANK], F32, name="acc%d" % n) for n in range(ROT_BANKS + 1)]
+
+        def mx_pass(g, n, w_words):
+            offset = 4 * (g % PLANES_PER_TILE)
+            nc.tensor.matmul_mx(
+                out=acc[n][:],
+                lhsT=x_codes[:, g * P : (g + 1) * P].bitcast(FP8X4),
+                lhsT_scale=x_scales[:, g * P : (g + 1) * P],
+                rhs=w_words.bitcast(FP8X4),
+                rhs_scale=plane_tiles[g // PLANES_PER_TILE][offset:P, n * BANK : (n + 1) * BANK],
+                start=(g == 0),
+                stop=(g == GROUPS - 1),
+            )
+
+        for g in range(GROUPS):
+            for n in range(ROT_BANKS):
+                mx_pass(g, n, qk_tiles[g][:, n * BANK : (n + 1) * BANK])
+            if g + QK_BUFS < GROUPS:
+                qk_tiles.append(load_qk(g + QK_BUFS))
+            elif g + QK_BUFS == GROUPS:
+                v_tiles.extend(load_v(i) for i in range(V_LOADS))
+
+        q_flat = out_0.rearrange("t h d -> t (h d)")
+        k_flat = out_1.rearrange("t h d -> t (h d)")
+        v_flat = out_2.rearrange("t h d -> t (h d)")
+        shape = [P, HEADS_PER_BANK, 2, D]
+        for n in range(ROT_BANKS):
+            prod = prod_pool.tile(shape, F32, name="prod")
+            nc.vector.tensor_tensor(
+                out=prod[:],
+                in0=acc[n][:].rearrange("p (h c) -> p h c", h=HEADS_PER_BANK).unsqueeze(2).to_broadcast(shape),
+                in1=rotation[:].unsqueeze(1).to_broadcast(shape),
+                op=ALU.mult,
+            )
+            rotated = out_pool.tile([P, BANK], F32, name="result")
+            terms = prod[:].rearrange("p h a (i b) -> p h i a b", b=2)
+            nc.vector.tensor_tensor(
+                out=rotated[:].rearrange("p (h i a) -> p h i a", h=HEADS_PER_BANK, a=2),
+                in0=terms[:, :, :, :, 0],
+                in1=terms[:, :, :, :, 1],
+                op=ALU.add,
+            )
+            if n * BANK < q_flat.shape[1]:
+                nc.sync.dma_start(out=q_flat[:, n * BANK : (n + 1) * BANK], in_=rotated[:])
+            else:
+                nc.sync.dma_start(out=k_flat, in_=rotated[:])
+
+        for g in range(GROUPS):
+            mx_pass(g, ROT_BANKS, v_tiles[g // V_GROUPS_PER_LOAD][:, g % V_GROUPS_PER_LOAD, :])
+        v_result = out_pool.tile([P, BANK], F32, name="result")
+        nc.scalar.copy(out=v_result[:], in_=acc[ROT_BANKS][:])
+        nc.sync.dma_start(out=v_flat, in_=v_result[:])

@@ -58,6 +58,9 @@ def tile_attention_pa_k_kernel(tc, x, w_qkv_words, w_qkv_scales, out_0, out_1, o
         xt_psum = ctx.enter_context(tc.psum_pool(name="xt_psum", bufs=2))
         acc_psum = ctx.enter_context(tc.psum_pool(name="acc_psum", bufs=1))
 
+        ident = const.tile([P, P], F32, name="ident")
+        make_identity(nc, ident[:])
+
         x_chunks = []
         chunk_cols = GROUPS_PER_CHUNK * K_PASS
         for c in range(X_CHUNKS):
@@ -72,11 +75,11 @@ def tile_attention_pa_k_kernel(tc, x, w_qkv_words, w_qkv_scales, out_0, out_1, o
             plane_tiles.append(planes)
         for j in range(PLANE_TILES):
             for quadrant in range(4):
-                nc.sync.dma_start(
-                    out=plane_tiles[j][32 * quadrant : 32 * quadrant + 16, :].bitcast(I32),
+                nc.gpsimd.dma_start(
+                    out=plane_tiles[j][32 * quadrant : 32 * quadrant + 16, :].bitcast(F32),
                     in_=w_qkv_scales[
                         PLANES_PER_TILE * j : PLANES_PER_TILE * (j + 1), 4 * quadrant : 4 * quadrant + 4, :
-                    ].bitcast(I32),
+                    ].bitcast(F32),
                 )
 
         def load_qk(g):
@@ -96,8 +99,6 @@ def tile_attention_pa_k_kernel(tc, x, w_qkv_words, w_qkv_scales, out_0, out_1, o
         qk_tiles = [load_qk(g) for g in range(QK_BUFS)]
         v_tiles = []
 
-        ident = const.tile([P, P], F32, name="ident")
-        make_identity(nc, ident[:])
         x_codes = const.tile([P, GROUPS * P], U32, name="x_codes", align_bytes=64)
         x_scales = const.tile([P, GROUPS * P], U8, name="x_scales", align_bytes=64)
         fill_cols = GROUPS_PER_FILL * P

@@ -32,9 +32,10 @@ GROUPS_PER_FILL = 2
 FILLS = GROUPS // GROUPS_PER_FILL
 PLANES_PER_TILE = 4
 PLANE_TILES = GROUPS // PLANES_PER_TILE
-QK_BUFS = 8
+QK_BUFS = 12
 V_GROUPS_PER_LOAD = 2
-V_LOADS = GROUPS // V_GROUPS_PER_LOAD
+V_PAIRED_GROUPS = 14
+V_HALF = BANK // 2
 
 TWO_PI = 2.0 * math.pi
 TWO_PI_HIGH = 6.28125
@@ -50,11 +51,11 @@ def tile_attention_pa_k_kernel(tc, x, w_qkv_words, w_qkv_scales, out_0, out_1, o
         ctx.enter_context(tc.manual_schedule())
         const = ctx.enter_context(tc.tile_pool(name="const", bufs=1))
         x_pool = ctx.enter_context(tc.tile_pool(name="x_pool", bufs=X_CHUNKS))
-        grouped_pool = ctx.enter_context(tc.tile_pool(name="grouped_pool", bufs=4))
+        grouped_pool = ctx.enter_context(tc.tile_pool(name="grouped_pool", bufs=2))
         qk_pool = ctx.enter_context(tc.tile_pool(name="qk_pool", bufs=QK_BUFS))
-        v_pool = ctx.enter_context(tc.tile_pool(name="v_pool", bufs=V_LOADS))
+        v_pool = ctx.enter_context(tc.tile_pool(name="v_pool", bufs=1))
         prod_pool = ctx.enter_context(tc.tile_pool(name="prod_pool", bufs=2))
-        out_pool = ctx.enter_context(tc.tile_pool(name="out_pool", bufs=ROT_BANKS + 1))
+        out_pool = ctx.enter_context(tc.tile_pool(name="out_pool", bufs=ROT_BANKS))
         xt_psum = ctx.enter_context(tc.psum_pool(name="xt_psum", bufs=2))
         acc_psum = ctx.enter_context(tc.psum_pool(name="acc_psum", bufs=1))
 
@@ -88,16 +89,19 @@ def tile_attention_pa_k_kernel(tc, x, w_qkv_words, w_qkv_scales, out_0, out_1, o
             nc.sync.dma_start(out=w_qk[:].bitcast(I32), in_=words[:, 0 : 4 * N_ROT].bitcast(I32))
             return w_qk
 
-        def load_v(i):
-            w_v = v_pool.tile([P, V_GROUPS_PER_LOAD, BANK], U32, name="w_v", align_bytes=64)
-            words = w_qkv_words[V_GROUPS_PER_LOAD * i : V_GROUPS_PER_LOAD * (i + 1)].rearrange(
-                "g p n t -> p g (n t)"
-            )
-            nc.sync.dma_start(out=w_v[:].bitcast(I32), in_=words[:, :, 4 * N_ROT : 4 * N_ALL].bitcast(I32))
-            return w_v
+        v_words = {}
+
+        def load_v(first_group, groups, first_half, halves):
+            cols = halves * V_HALF
+            w_v = v_pool.tile([P, groups, cols], U32, name="w_v_%d_%d" % (first_group, first_half), align_bytes=64)
+            words = w_qkv_words[first_group : first_group + groups].rearrange("g p n t -> p g (n t)")
+            first_byte = 4 * (N_ROT + first_half * V_HALF)
+            nc.sync.dma_start(out=w_v[:].bitcast(I32), in_=words[:, :, first_byte : first_byte + 4 * cols].bitcast(I32))
+            for i in range(groups):
+                for h in range(halves):
+                    v_words[(first_group + i, first_half + h)] = w_v[:, i, h * V_HALF : (h + 1) * V_HALF]
 
         qk_tiles = [load_qk(g) for g in range(QK_BUFS)]
-        v_tiles = []
 
         x_codes = const.tile([P, GROUPS * P], U32, name="x_codes", align_bytes=64)
         x_scales = const.tile([P, GROUPS * P], U8, name="x_scales", align_bytes=64)
@@ -182,27 +186,31 @@ def tile_attention_pa_k_kernel(tc, x, w_qkv_words, w_qkv_scales, out_0, out_1, o
             out=rotation[:].rearrange("p a c -> p (a c)"), in_=reduced[:], func=mybir.ActivationFunctionType.Sin
         )
 
-        acc = [acc_psum.tile([P, BANK], F32, name="acc%d" % n) for n in range(ROT_BANKS + 1)]
+        acc = [acc_psum.tile([P, BANK], F32, name="acc%d" % n) for n in range(ROT_BANKS)]
 
-        def mx_pass(g, n, w_words):
+        def mx_pass(g, total, first_col, w_words):
             offset = 4 * (g % PLANES_PER_TILE)
             nc.tensor.matmul_mx(
-                out=acc[n][:],
+                out=total,
                 lhsT=x_codes[:, g * P : (g + 1) * P].bitcast(FP8X4),
                 lhsT_scale=x_scales[:, g * P : (g + 1) * P],
                 rhs=w_words.bitcast(FP8X4),
-                rhs_scale=plane_tiles[g // PLANES_PER_TILE][offset:P, n * BANK : (n + 1) * BANK],
+                rhs_scale=plane_tiles[g // PLANES_PER_TILE][offset:P, first_col : first_col + total.shape[1]],
                 start=(g == 0),
                 stop=(g == GROUPS - 1),
             )
 
         for g in range(GROUPS):
             for n in range(ROT_BANKS):
-                mx_pass(g, n, qk_tiles[g][:, n * BANK : (n + 1) * BANK])
+                mx_pass(g, acc[n][:], n * BANK, qk_tiles[g][:, n * BANK : (n + 1) * BANK])
             if g + QK_BUFS < GROUPS:
                 qk_tiles.append(load_qk(g + QK_BUFS))
             elif g + QK_BUFS == GROUPS:
-                v_tiles.extend(load_v(i) for i in range(V_LOADS))
+                for first_group in range(0, V_PAIRED_GROUPS, V_GROUPS_PER_LOAD):
+                    load_v(first_group, V_GROUPS_PER_LOAD, 0, 2)
+                load_v(V_PAIRED_GROUPS, 1, 0, 2)
+                load_v(GROUPS - 1, 1, 0, 1)
+                load_v(GROUPS - 1, 1, 1, 1)
 
         q_flat = out_0.rearrange("t h d -> t (h d)")
         k_flat = out_1.rearrange("t h d -> t (h d)")
@@ -229,8 +237,11 @@ def tile_attention_pa_k_kernel(tc, x, w_qkv_words, w_qkv_scales, out_0, out_1, o
             else:
                 nc.sync.dma_start(out=k_flat, in_=rotated[:])
 
+        v_acc = [acc_psum.tile([P, V_HALF], F32, name="v_acc0"), xt_psum.tile([P, V_HALF], F32, name="xt")]
         for g in range(GROUPS):
-            mx_pass(g, ROT_BANKS, v_tiles[g // V_GROUPS_PER_LOAD][:, g % V_GROUPS_PER_LOAD, :])
-        v_result = out_pool.tile([P, BANK], F32, name="result")
-        nc.scalar.copy(out=v_result[:], in_=acc[ROT_BANKS][:])
-        nc.sync.dma_start(out=v_flat, in_=v_result[:])
+            for h in range(2):
+                mx_pass(g, v_acc[h][:], N_ROT + h * V_HALF, v_words[(g, h)])
+        for h in range(2):
+            v_result = out_pool.tile([P, V_HALF], F32, name="v_result")
+            nc.scalar.copy(out=v_result[:], in_=v_acc[h][:])
+            nc.scalar.dma_start(out=v_flat[:, h * V_HALF : (h + 1) * V_HALF], in_=v_result[:])

@@ -54,7 +54,7 @@ def tile_attention_pa_k_kernel(tc, x, w_qkv_words, w_qkv_scales, out_0, out_1, o
         grouped_pool = ctx.enter_context(tc.tile_pool(name="grouped_pool", bufs=2))
         qk_pool = ctx.enter_context(tc.tile_pool(name="qk_pool", bufs=QK_BUFS))
         v_pool = ctx.enter_context(tc.tile_pool(name="v_pool", bufs=1))
-        prod_pool = ctx.enter_context(tc.tile_pool(name="prod_pool", bufs=2))
+        prod_pool = ctx.enter_context(tc.tile_pool(name="prod_pool", bufs=3))
         out_pool = ctx.enter_context(tc.tile_pool(name="out_pool", bufs=ROT_BANKS))
         xt_psum = ctx.enter_context(tc.psum_pool(name="xt_psum", bufs=2))
         acc_psum = ctx.enter_context(tc.psum_pool(name="acc_psum", bufs=1))
@@ -226,7 +226,7 @@ def tile_attention_pa_k_kernel(tc, x, w_qkv_words, w_qkv_scales, out_0, out_1, o
             )
             rotated = out_pool.tile([P, BANK], F32, name="result")
             terms = prod[:].rearrange("p h a (i b) -> p h i a b", b=2)
-            nc.vector.tensor_tensor(
+            nc.gpsimd.tensor_tensor(
                 out=rotated[:].rearrange("p (h i a) -> p h i a", h=HEADS_PER_BANK, a=2),
                 in0=terms[:, :, :, :, 0],
                 in1=terms[:, :, :, :, 1],

import math
from contextlib import ExitStack

import concourse.mybir as mybir
from concourse.masks import make_identity

F32 = mybir.dt.float32
BF16 = mybir.dt.bfloat16
I32 = mybir.dt.int32
U32 = mybir.dt.uint32
U8 = mybir.dt.uint8
FP8X4 = mybir.dt.float8_e4m3fn_x4
ALU = mybir.AluOpType

P = 128
DIM = 8192
K_PASS = 512
GROUPS = DIM // K_PASS
D = 128
HALF = D // 2
DOUBLINGS = 6
BANK = 512
HEADS_PER_BANK = BANK // D
N_ALL = 3072
N_ROT = 2560
ROT_BANKS = N_ROT // BANK
THETA = 10000.0

X_CHUNKS = 4
GROUPS_PER_CHUNK = GROUPS // X_CHUNKS
GROUPS_PER_FILL = 2
FILLS = GROUPS // GROUPS_PER_FILL
PLANES_PER_TILE = 4
PLANE_TILES = GROUPS // PLANES_PER_TILE
QK_BUFS = 12
V_GROUPS_PER_LOAD = 2
V_PAIRED_GROUPS = 14
V_HALF = BANK // 2

TWO_PI = 2.0 * math.pi
TWO_PI_HIGH = 6.28125
TWO_PI_LOW = TWO_PI - TWO_PI_HIGH
ROUND_MAGIC = 12582912.0

FLOPS = 2 * P * DIM * N_ALL


def tile_attention_pa_k_kernel(tc, x, w_qkv_words, w_qkv_scales, out_0, out_1, out_2):
    nc = tc.nc
    with ExitStack() as ctx:
        ctx.enter_context(tc.manual_schedule())
        const = ctx.enter_context(tc.tile_pool(name="const", bufs=1))
        x_pool = ctx.enter_context(tc.tile_pool(name="x_pool", bufs=X_CHUNKS))
        grouped_pool = ctx.enter_context(tc.tile_pool(name="grouped_pool", bufs=2))
        qk_pool = ctx.enter_context(tc.tile_pool(name="qk_pool", bufs=QK_BUFS))
        v_pool = ctx.enter_context(tc.tile_pool(name="v_pool", bufs=1))
        prod_pool = ctx.enter_context(tc.tile_pool(name="prod_pool", bufs=3))
        out_pool = ctx.enter_context(tc.tile_pool(name="out_pool", bufs=ROT_BANKS))
        xt_psum = ctx.enter_context(tc.psum_pool(name="xt_psum", bufs=2))
        acc_psum = ctx.enter_context(tc.psum_pool(name="acc_psum", bufs=1))

        ident = const.tile([P, P], F32, name="ident")
        make_identity(nc, ident[:])

        x_chunks = []
        chunk_cols = GROUPS_PER_CHUNK * K_PASS
        for c in range(X_CHUNKS):
            x_chunk = x_pool.tile([P, chunk_cols], BF16, name="x_chunk")
            nc.sync.dma_start(out=x_chunk[:], in_=x[:, c * chunk_cols : (c + 1) * chunk_cols])
            x_chunks.append(x_chunk)

        plane_tiles = []
        for j in range(PLANE_TILES):
            planes = const.tile([P, N_ALL], U8, name="planes%d" % j, align_bytes=64)
            nc.vector.memset(planes[:].bitcast(I32), 0)
            plane_tiles.append(planes)
        for j in range(PLANE_TILES):
            for quadrant in range(4):
                nc.gpsimd.dma_start(
                    out=plane_tiles[j][32 * quadrant : 32 * quadrant + 16, :].bitcast(F32),
                    in_=w_qkv_scales[
                        PLANES_PER_TILE * j : PLANES_PER_TILE * (j + 1), 4 * quadrant : 4 * quadrant + 4, :
                    ].bitcast(F32),
                )

        def load_qk(g):
            w_qk = qk_pool.tile([P, N_ROT], U32, name="w_qk", align_bytes=64)
            words = w_qkv_words[g].rearrange("p n t -> p (n t)")
            nc.sync.dma_start(out=w_qk[:].bitcast(I32), in_=words[:, 0 : 4 * N_ROT].bitcast(I32))
            return w_qk

        v_words = {}

        def load_v(first_group, groups, first_half, halves):
            cols = halves * V_HALF
            w_v = v_pool.tile([P, groups, cols], U32, name="w_v_%d_%d" % (first_group, first_half), align_bytes=64)
            words = w_qkv_words[first_group : first_group + groups].rearrange("g p n t -> p g (n t)")
            first_byte = 4 * (N_ROT + first_half * V_HALF)
            nc.sync.dma_start(out=w_v[:].bitcast(I32), in_=words[:, :, first_byte : first_byte + 4 * cols].bitcast(I32))
            for i in range(groups):
                for h in range(halves):
                    v_words[(first_group + i, first_half + h)] = w_v[:, i, h * V_HALF : (h + 1) * V_HALF]

        qk_tiles = [load_qk(g) for g in range(QK_BUFS)]

        x_codes = const.tile([P, GROUPS * P], U32, name="x_codes", align_bytes=64)
        x_scales = const.tile([P, GROUPS * P], U8, name="x_scales", align_bytes=64)
        fill_cols = GROUPS_PER_FILL * P

        def quantise_fill(b, grouped):
            cols = slice(b * fill_cols, (b + 1) * fill_cols)
            nc.vector.quantize_mx(out=x_codes[:, cols].bitcast(FP8X4), scales=x_scales[:, cols], in_=grouped[:])

        previous = None
        for b in range(FILLS):
            xt = xt_psum.tile([P, GROUPS_PER_FILL, 2, P], F32, name="xt")
            for i in range(GROUPS_PER_FILL):
                g = GROUPS_PER_FILL * b + i
                words = x_chunks[g // GROUPS_PER_CHUNK][:].bitcast(F32)
                first = (g % GROUPS_PER_CHUNK) * (K_PASS // 2)
                for u in range(2):
                    nc.tensor.transpose(
                        xt[:, i, u, :], words[:, first + u : first + K_PASS // 2 : 2], ident[:]
                    )
            grouped = grouped_pool.tile([P, 4 * fill_cols], BF16, name="grouped", align_bytes=64)
            grouped_words = grouped[:].bitcast(F32).rearrange("p (i r u) -> p i r u", i=GROUPS_PER_FILL, u=2)
            xt_words = xt[:].rearrange("p i u r -> p i r u")
            if b % 2 == 0:
                nc.vector.tensor_copy(out=grouped_words, in_=xt_words)
            else:
                nc.scalar.copy(out=grouped_words, in_=xt_words)
            if previous is not None:
                quantise_fill(b - 1, previous)
            previous = grouped
        quantise_fill(FILLS - 1, previous)

        pos_int = const.tile([P, 1], I32, name="pos_int")
        nc.gpsimd.iota(pos_int[:], pattern=[[0, 1]], base=0, channel_multiplier=1)
        pos = const.tile([P, 1], F32, name="pos")
        nc.vector.tensor_copy(out=pos[:], in_=pos_int[:])
        neg_pos = const.tile([P, 1], F32, name="neg_pos")
        nc.vector.tensor_scalar(out=neg_pos[:], in0=pos[:], scalar1=-1.0, scalar2=None, op0=ALU.mult)
        freq = const.tile([P, HALF], F32, name="freq")
        nc.vector.memset(freq[:, 0:1], 1.0)
        for doubling in range(DOUBLINGS):
            span = 2**doubling
            nc.vector.tensor_scalar(
                out=freq[:, span : 2 * span],
                in0=freq[:, 0:span],
                scalar1=THETA ** (-2.0 * span / D),
                scalar2=None,
                op0=ALU.mult,
            )
        angle = const.tile([P, 2, HALF, 2], F32, name="angle")

        def angle_plane(row, col, position, shift):
            nc.vector.tensor_scalar(
                out=angle[:, row, :, col],
                in0=freq[:],
                scalar1=position[:],
                scalar2=shift,
                op0=ALU.mult,
                op1=ALU.add,
            )

        angle_plane(0, 0, pos, math.pi / 2)
        angle_plane(0, 1, neg_pos, 0.0)
        angle_plane(1, 0, pos, 0.0)
        angle_plane(1, 1, pos, math.pi / 2)
        angle_flat = angle[:].rearrange("p a i b -> p (a i b)")
        turns = const.tile([P, 4 * HALF], F32, name="turns")
        nc.vector.tensor_scalar(
            out=turns[:], in0=angle_flat, scalar1=1.0 / TWO_PI, scalar2=ROUND_MAGIC, op0=ALU.mult, op1=ALU.add
        )
        nc.vector.tensor_scalar(out=turns[:], in0=turns[:], scalar1=ROUND_MAGIC, scalar2=None, op0=ALU.subtract)
        reduced_high = const.tile([P, 4 * HALF], F32, name="reduced_high")
        nc.vector.scalar_tensor_tensor(
            out=reduced_high[:], in0=turns[:], scalar=-TWO_PI_HIGH, in1=angle_flat, op0=ALU.mult, op1=ALU.add
        )
        reduced = const.tile([P, 4 * HALF], F32, name="reduced")
        nc.vector.scalar_tensor_tensor(
            out=reduced[:], in0=turns[:], scalar=-TWO_PI_LOW, in1=reduced_high[:], op0=ALU.mult, op1=ALU.add
        )
        rotation = const.tile([P, 2, D], F32, name="rotation")
        nc.scalar.activation(
            out=rotation[:].rearrange("p a c -> p (a c)"), in_=reduced[:], func=mybir.ActivationFunctionType.Sin
        )

        acc = [acc_psum.tile([P, BANK], F32, name="acc%d" % n) for n in range(ROT_BANKS)]

        def mx_pass(g, total, first_col, w_words):
            offset = 4 * (g % PLANES_PER_TILE)
            nc.tensor.matmul_mx(
                out=total,
                lhsT=x_codes[:, g * P : (g + 1) * P].bitcast(FP8X4),
                lhsT_scale=x_scales[:, g * P : (g + 1) * P],
                rhs=w_words.bitcast(FP8X4),
                rhs_scale=plane_tiles[g // PLANES_PER_TILE][offset:P, first_col : first_col + total.shape[1]],
                start=(g == 0),
                stop=(g == GROUPS - 1),
            )

        for g in range(GROUPS):
            for n in range(ROT_BANKS):
                mx_pass(g, acc[n][:], n * BANK, qk_tiles[g][:, n * BANK : (n + 1) * BANK])
            if g + QK_BUFS < GROUPS:
                qk_tiles.append(load_qk(g + QK_BUFS))
            elif g + QK_BUFS == GROUPS:
                for first_group in range(0, V_PAIRED_GROUPS, V_GROUPS_PER_LOAD):
                    load_v(first_group, V_GROUPS_PER_LOAD, 0, 2)
                load_v(V_PAIRED_GROUPS, 1, 0, 2)
                load_v(GROUPS - 1, 1, 0, 1)
                load_v(GROUPS - 1, 1, 1, 1)

        q_flat = out_0.rearrange("t h d -> t (h d)")
        k_flat = out_1.rearrange("t h d -> t (h d)")
        v_flat = out_2.rearrange("t h d -> t (h d)")
        shape = [P, HEADS_PER_BANK, 2, D]
        for n in range(ROT_BANKS):
            prod = prod_pool.tile(shape, F32, name="prod")
            nc.vector.tensor_tensor(
                out=prod[:],
                in0=acc[n][:].rearrange("p (h c) -> p h c", h=HEADS_PER_BANK).unsqueeze(2).to_broadcast(shape),
                in1=rotation[:].unsqueeze(1).to_broadcast(shape),
                op=ALU.mult,
            )
            rotated = out_pool.tile([P, BANK], F32, name="result")
            terms = prod[:].rearrange("p h a (i b) -> p h i a b", b=2)
            nc.gpsimd.tensor_tensor(
                out=rotated[:].rearrange("p (h i a) -> p h i a", h=HEADS_PER_BANK, a=2),
                in0=terms[:, :, :, :, 0],
                in1=terms[:, :, :, :, 1],
                op=ALU.add,
            )
            if n * BANK < q_flat.shape[1]:
                nc.sync.dma_start(out=q_flat[:, n * BANK : (n + 1) * BANK], in_=rotated[:])
            else:
                nc.sync.dma_start(out=k_flat, in_=rotated[:])

        v_acc = [acc_psum.tile([P, V_HALF], F32, name="v_acc0"), xt_psum.tile([P, V_HALF], F32, name="xt")]
        for g in range(GROUPS):
            for h in range(2):
                mx_pass(g, v_acc[h][:], N_ROT + h * V_HALF, v_words[(g, h)])
        for h in range(2):
            v_result = out_pool.tile([P, V_HALF], F32, name="v_result")
            nc.scalar.copy(out=v_result[:], in_=v_acc[h][:])
            nc.scalar.dma_start(out=v_flat[:, h * V_HALF : (h + 1) * V_HALF], in_=v_result[:])
